import numpy as np
import ml_dtypes


def mxq(x, axis, fmt="e4m3"):
    dtype, down = {"e4m3": (ml_dtypes.float8_e4m3fn, 7), "e5m2": (ml_dtypes.float8_e5m2, 14)}[fmt]
    v = np.moveaxis(np.asarray(x, np.float32).astype(ml_dtypes.bfloat16).astype(np.float64), axis, -1)
    blocks = v.reshape(v.shape[:-1] + (-1, 32))
    amax = np.abs(blocks).max(-1, keepdims=True)
    byte = np.maximum(np.where(amax > 0, np.frexp(amax)[1] - 1 + 127, 0) - down, 1)
    scale = np.exp2(byte - 127.0)
    codes = (blocks / scale).astype(np.float32).astype(dtype).astype(np.float64)
    return np.moveaxis((codes * scale).reshape(v.shape), -1, axis)


WIDE = False


def mx_kscale(k):
    if not WIDE:
        return np.ones(k)
    levels = np.array([10, -10, 5, -5, 0])
    if k % 512:
        return np.exp2(np.random.permutation(np.resize(levels, k // 32))).repeat(32)
    a = np.empty((k // 512, 16))
    for p in range(k // 512):
        a[p, :8] = np.random.permutation(np.resize(levels, 8))
        for g in range(8):
            far = levels[np.abs(levels - a[p, g]) >= 10]
            a[p, g + 8] = far[np.random.randint(len(far))]
    return np.exp2(a.ravel()).repeat(32)


BF16 = ml_dtypes.bfloat16


def bf(x):
    return np.asarray(x, np.float32).astype(BF16)


def f64(x):
    return np.asarray(x).astype(np.float64)


IN, H, C, B = 1024, 512, 2, 1024
J = C * 2 * H


def sigmoid(v):
    return 1.0 / (1.0 + np.exp(-v))


def net_of(input_word, hidden_states, Wx, bx, Wh):
    px = f64(input_word) @ f64(Wx).reshape(C * 2 * H, IN).T
    ph = f64(hidden_states) @ f64(Wh).reshape(C * 2 * H, H).T
    return (px + ph).reshape(-1, C, 2 * H) + f64(bx)[None, :, :]


def setup_inputs():
    s = mx_kscale(B)
    u = mx_kscale(J).reshape(C, 2 * H)
    ug = np.concatenate([u[:, H:], u[:, :H]], axis=-1)
    x0 = bf(np.random.standard_normal((B, IN)))
    hs = bf(np.random.standard_normal((B, H)))
    Wx0 = bf(np.random.uniform(-1.0, 1.0, (C, 2 * H, IN)) / np.sqrt(IN))
    bx = bf(np.random.standard_normal((C, 2 * H)) * 0.3)
    Wh = bf(np.random.uniform(-1.0, 1.0, (C, 2 * H, H)) / np.sqrt(H))
    g = bf(np.random.standard_normal((B, C, 2 * H)) * np.exp2(np.random.randint(-6, 1, (B, 1, 1))) * 4.0
           / s[:, None, None] * ug[None, :, :])
    net = net_of(x0, hs, Wx0, bx, Wh)
    return {"input_word": bf(f64(x0) * s[:, None]), "hidden_states": hs, "Wx": bf(f64(Wx0) / u[:, :, None]),
            "bx": bx, "Wh": Wh, "net": np.asarray(net, np.float32), "grad_out": g}


def reference(input_word, hidden_states, Wx, bx, Wh, net, grad_out):
    n = f64(net)
    g = f64(grad_out)
    sg = sigmoid(n[..., :H])
    th = np.tanh(n[..., H:])
    d_gate = g[..., H:] * (sg * (1.0 - sg))
    d_cell = g[..., :H] * (1.0 - th * th)
    dnet = np.concatenate([d_gate, d_cell], axis=-1).reshape(B, J)
    w2 = f64(Wx).reshape(J, IN)
    dx = mxq(dnet, 1, "e5m2") @ mxq(w2, 0, "e4m3")
    dw = mxq(dnet, 0, "e5m2").T @ mxq(f64(input_word), 0, "e4m3")
    return dx, dw.reshape(C, 2 * H, IN)

@@ -1,0 +1,225 @@
+from contextlib import ExitStack
+
+import concourse.mybir as mybir
+from concourse.masks import make_identity
+
+B, IN, J = 1024, 1024, 2048
+FLOPS = 2 * 2 * B * J * IN
+BYTES = B * J * 4 + B * J * 2 + J * IN * 2 + B * IN * 2 + B * IN * 4 + J * IN * 4
+
+F32 = mybir.dt.float32
+BF16 = mybir.dt.bfloat16
+U32 = mybir.dt.uint32
+U8 = mybir.dt.uint8
+E4 = mybir.dt.float8_e4m3fn_x4
+E5 = mybir.dt.float8_e5m2_x4
+ACT = mybir.ActivationFunctionType
+ALU = mybir.AluOpType
+
+P = 128
+PACK = 4
+KP = P * PACK
+NT = 512
+
+
+def tile_compute_gate_v_kernel(tc, input_word, hidden_states, Wx, bx, Wh, net, grad_out, out_0, out_1):
+    nc = tc.nc
+
+    net_v = net.rearrange("(g p j) c h -> g j p (c h)", g=2, p=P, j=PACK)
+    grad_v = grad_out.rearrange("(g p j) c h -> g j p (c h)", g=2, p=P, j=PACK)
+    x_v = input_word.rearrange("(g p j) n -> g p j n", g=2, p=P, j=PACK)
+    w_v = Wx.rearrange("c (a p j) n -> (c a) p j n", a=2, p=P, j=PACK)
+    out0_v = out_0.rearrange("(g r j) n -> g j r n", g=2, r=P, j=PACK)
+    out1_v = out_1.rearrange("c (m p) n -> (c m) p n", p=P)
+
+    with ExitStack() as ctx:
+        raw = ctx.enter_context(tc.tile_pool(name="raw", bufs=10))
+        keep = ctx.enter_context(tc.tile_pool(name="keep", bufs=1))
+        grp = ctx.enter_context(tc.tile_pool(name="grp", bufs=2))
+        outp = ctx.enter_context(tc.tile_pool(name="outp", bufs=4))
+        psum = ctx.enter_context(tc.psum_pool(name="psum", bufs=8))
+
+        xq = keep.tile([P, 2, IN], U32, name="xq", align_bytes=64)
+        xs = keep.tile([P, 2, IN], U8, name="xs", align_bytes=64)
+        wq = keep.tile([P, 4, IN], U32, name="wq", align_bytes=64)
+        ws = keep.tile([P, 4, IN], U8, name="ws", align_bytes=64)
+        tq = keep.tile([P, 2, J], U32, name="tq", align_bytes=64)
+        ts = keep.tile([P, 2, J], U8, name="ts", align_bytes=64)
+        fq = keep.tile([P, 8, KP], U32, name="fq", align_bytes=64)
+        fs = keep.tile([P, 8, KP], U8, name="fs", align_bytes=64)
+        dz0 = keep.tile([P, PACK, J], BF16, name="dz0", align_bytes=64)
+        dz1 = keep.tile([P, PACK, J], BF16, name="dz1", align_bytes=64)
+        dz = [dz0, dz1]
+        ident = keep.tile([P, P], F32, name="ident")
+        warm = keep.tile([P, 1], F32, name="warm")
+
+        nc.vector.memset(warm[:], 0.0)
+        nc.scalar.activation(out=warm[:], in_=warm[:], func=ACT.Tanh)
+        make_identity(nc, ident[:])
+
+        net_t = {}
+        x_t = {}
+        w_t = {}
+
+        def load_net(G, j, pieces):
+            t = raw.tile([P, J], F32, name="net_t", tag="raw")
+            step = J // pieces
+            for i in range(pieces):
+                nc.sync.dma_start(out=t[:, step * i : step * (i + 1)], in_=net_v[G, j][:, step * i : step * (i + 1)])
+            net_t[(G, j)] = t
+
+        def load_g(G, j):
+            nc.sync.dma_start(out=dz[G][:, j, :], in_=grad_v[G, j])
+
+        def load_x(G):
+            t = raw.tile([P, PACK, IN], BF16, name="x_t", tag="raw")
+            nc.sync.dma_start(out=t[:], in_=x_v[G])
+            x_t[G] = t
+
+        def load_w(g, pieces):
+            t = raw.tile([P, PACK, IN], BF16, name="w_t", tag="raw")
+            step = IN // pieces
+            for i in range(pieces):
+                nc.sync.dma_start(out=t[:, :, step * i : step * (i + 1)], in_=w_v[g][:, :, step * i : step * (i + 1)])
+            w_t[g] = t
+
+        def interleave(src, tag):
+            grouped = grp.tile([P, NT, PACK], BF16, name=tag, tag=tag, align_bytes=64)
+            nc.vector.tensor_copy(out=grouped[:], in_=src.rearrange("p j w -> p w j"))
+            return grouped
+
+        def quantize(grouped, codes, scales, fmt):
+            nc.vector.quantize_mx(out=codes.bitcast(fmt), scales=scales, in_=grouped[:].rearrange("p w j -> p (w j)"))
+
+        def quantize_pair(src, codes, scales, fmt, tag):
+            halves = [slice(NT * h, NT * (h + 1)) for h in range(2)]
+            grouped = [interleave(src[:, :, cols], tag) for cols in halves]
+            for h in range(2):
+                quantize(grouped[h], codes[:, halves[h]], scales[:, halves[h]], fmt)
+
+        def evict(on_vector, dst, acc):
+            if on_vector:
+                nc.vector.tensor_scalar_mul(out=dst, in0=acc[:], scalar1=-1.0)
+            else:
+                nc.scalar.mul(out=dst, in_=acc[:], mul=-1.0)
+
+        def activations(G, j):
+            halves = net_t[(G, j)][:].rearrange("p (c s w) -> p c s w", c=2, s=2)
+            for func in (ACT.Tanh, ACT.Square):
+                for s in range(2):
+                    nc.scalar.activation(out=halves[:, :, s, :], in_=halves[:, :, s, :], func=func, scale=0.5 if s == 0 else 1.0)
+
+        def multiply(G, j):
+            halves = net_t[(G, j)][:].rearrange("p (c s w) -> p c s w", c=2, s=2)
+            grads = dz[G][:, j, :].rearrange("p (c s w) -> p c s w", c=2, s=2)
+            for s in range(2):
+                nc.vector.scalar_tensor_tensor(
+                    out=grads[:, :, 1 - s, :],
+                    in0=halves[:, :, s, :],
+                    scalar=0.25 if s == 0 else 1.0,
+                    in1=grads[:, :, 1 - s, :],
+                    op0=ALU.subtract,
+                    op1=ALU.mult,
+                )
+
+        def turn(G, j):
+            gf = grp.tile([P, PACK * KP], BF16, name="gf", tag="gf", align_bytes=64)
+            gf_words = gf[:].bitcast(F32)
+            for b in range(2):
+                xt = psum.tile([P, NT], F32, name="xt", tag="bank")
+                for gg in range(2):
+                    pos = (2 * b + gg) ^ 1
+                    words = dz[G][:, j, KP * pos : KP * (pos + 1)].bitcast(F32)
+                    for u in range(2):
+                        col = (2 * gg + u) * P
+                        nc.tensor.transpose(xt[:, col : col + P], words[:, u : KP // 2 : 2], ident[:])
+                nc.scalar.copy(
+                    out=gf_words[:, NT * b : NT * (b + 1)].rearrange("p (g r u) -> p g r u", g=2, r=P, u=2),
+                    in_=xt[:].rearrange("p (g u r) -> p g r u", g=2, u=2, r=P),
+                )
+            nc.vector.quantize_mx(out=fq[:, PACK * G + j, :].bitcast(E5), scales=fs[:, PACK * G + j, :], in_=gf[:])
+
+        def dx(G, j):
+            i = PACK * G + j
+            o = outp.tile([P, IN], F32, name="o", tag="o")
+            for h in range(2):
+                cols = slice(NT * h, NT * (h + 1))
+                acc = psum.tile([P, NT], F32, name="acc", tag="bank")
+                for g in range(4):
+                    nc.tensor.matmul_mx(
+                        out=acc[:],
+                        lhsT=fq[:, i, P * g : P * (g + 1)].bitcast(E5),
+                        lhsT_scale=fs[:, i, P * g : P * (g + 1)],
+                        rhs=wq[:, g, cols].bitcast(E4),
+                        rhs_scale=ws[:, g, cols],
+                        start=(g == 0),
+                        stop=(g == 3),
+                    )
+                evict(h == 1 and i >= 2, o[:, cols], acc)
+            nc.sync.dma_start(out=out0_v[G, j], in_=o[:])
+
+        def dw(f):
+            for mm in range(4):
+                j0 = KP * f + P * mm
+                o = outp.tile([P, IN], F32, name="o", tag="o")
+                for h in range(2):
+                    cols = slice(NT * h, NT * (h + 1))
+                    acc = psum.tile([P, NT], F32, name="acc", tag="bank")
+                    for G in range(2):
+                        nc.tensor.matmul_mx(
+                            out=acc[:],
+                            lhsT=tq[:, G, j0 : j0 + P].bitcast(E5),
+                            lhsT_scale=ts[:, G, j0 : j0 + P],
+                            rhs=xq[:, G, cols].bitcast(E4),
+                            rhs_scale=xs[:, G, cols],
+                            start=(G == 0),
+                            stop=(G == 1),
+                        )
+                    evict(h == 1 and mm == 3, o[:, cols], acc)
+                nc.sync.dma_start(out=out1_v[4 * f + mm], in_=o[:])
+
+        load_net(0, 0, 2)
+        load_w(0, 2)
+        load_g(0, 0)
+        load_net(0, 1, 1)
+        load_w(1, 1)
+        load_g(0, 1)
+        load_net(0, 2, 1)
+        load_w(2, 1)
+        load_g(0, 2)
+        load_net(0, 3, 1)
+        load_w(3, 1)
+        load_g(0, 3)
+        load_net(1, 0, 1)
+        load_g(1, 0)
+        load_net(1, 1, 1)
+        load_g(1, 1)
+
+        for g in range(4):
+            quantize_pair(w_t[g], wq[:, g, :], ws[:, g, :], E4, "gw")
+
+        for G in range(2):
+            for j in range(4):
+                activations(G, j)
+                multiply(G, j)
+                turn(G, j)
+                dx(G, j)
+                if (G, j) == (0, 0):
+                    load_x(0)
+                    load_net(1, 2, 1)
+                    load_g(1, 2)
+                if (G, j) == (0, 1):
+                    load_x(1)
+                    load_net(1, 3, 1)
+                    load_g(1, 3)
+                if (G, j) == (0, 3):
+                    quantize_pair(x_t[0], xq[:, 0, :], xs[:, 0, :], E4, "gw")
+                if (G, j) == (1, 1):
+                    quantize_pair(x_t[1], xq[:, 1, :], xs[:, 1, :], E4, "gw")
+
+        for f in range(4):
+            pos = f ^ 1
+            grouped = [interleave(dz[G][:, :, KP * pos : KP * (pos + 1)], "gt") for G in range(2)]
+            for G in range(2):
+                quantize(grouped[G], tq[:, G, KP * f : KP * (f + 1)], ts[:, G, KP * f : KP * (f + 1)], E5)
+            dw(f)

@@ -20,6 +20,8 @@ P = 128
 PACK = 4
 KP = P * PACK
 NT = 512
+LEAD = 2
+FILL = [1, 2, 2, 1, 1, 2, 1, 0]
 
 
 def tile_compute_gate_v_kernel(tc, input_word, hidden_states, Wx, bx, Wh, net, grad_out, out_0, out_1):
@@ -57,45 +59,53 @@ def tile_compute_gate_v_kernel(tc, input_word, hidden_states, Wx, bx, Wh, net, g
         nc.scalar.activation(out=warm[:], in_=warm[:], func=ACT.Tanh)
         make_identity(nc, ident[:])
 
-        net_t = {}
-        x_t = {}
-        w_t = {}
+        ctx.enter_context(tc.manual_schedule())
 
-        def load_net(G, j, pieces):
+        net_t = {}
+        raw_t = {}
+        grouped_t = {}
+        xt_t = {}
+        gf_t = {}
+        acc_t = {}
+
+        def load_net(k, pieces):
             t = raw.tile([P, J], F32, name="net_t", tag="raw")
             step = J // pieces
             for i in range(pieces):
-                nc.sync.dma_start(out=t[:, step * i : step * (i + 1)], in_=net_v[G, j][:, step * i : step * (i + 1)])
-            net_t[(G, j)] = t
+                nc.sync.dma_start(out=t[:, step * i : step * (i + 1)], in_=net_v[k // 4, k % 4][:, step * i : step * (i + 1)])
+            net_t[k] = t
 
-        def load_g(G, j):
-            nc.sync.dma_start(out=dz[G][:, j, :], in_=grad_v[G, j])
+        def load_g(k):
+            nc.sync.dma_start(out=dz[k // 4][:, k % 4, :], in_=grad_v[k // 4, k % 4])
 
-        def load_x(G):
-            t = raw.tile([P, PACK, IN], BF16, name="x_t", tag="raw")
-            nc.sync.dma_start(out=t[:], in_=x_v[G])
-            x_t[G] = t
-
-        def load_w(g, pieces):
-            t = raw.tile([P, PACK, IN], BF16, name="w_t", tag="raw")
+        def load_rows(kind, a, view, pieces):
+            t = raw.tile([P, PACK, IN], BF16, name="rows_t", tag="raw")
             step = IN // pieces
             for i in range(pieces):
-                nc.sync.dma_start(out=t[:, :, step * i : step * (i + 1)], in_=w_v[g][:, :, step * i : step * (i + 1)])
-            w_t[g] = t
+                nc.sync.dma_start(out=t[:, :, step * i : step * (i + 1)], in_=view[a][:, :, step * i : step * (i + 1)])
+            raw_t[(kind, a)] = t
 
-        def interleave(src, tag):
+        def interleave(key, src, tag):
             grouped = grp.tile([P, NT, PACK], BF16, name=tag, tag=tag, align_bytes=64)
             nc.vector.tensor_copy(out=grouped[:], in_=src.rearrange("p j w -> p w j"))
-            return grouped
+            grouped_t[key] = grouped
 
-        def quantize(grouped, codes, scales, fmt):
-            nc.vector.quantize_mx(out=codes.bitcast(fmt), scales=scales, in_=grouped[:].rearrange("p w j -> p (w j)"))
+        def quantize(key, codes, scales, fmt):
+            nc.vector.quantize_mx(out=codes.bitcast(fmt), scales=scales, in_=grouped_t[key][:].rearrange("p w j -> p (w j)"))
 
-        def quantize_pair(src, codes, scales, fmt, tag):
-            halves = [slice(NT * h, NT * (h + 1)) for h in range(2)]
-            grouped = [interleave(src[:, :, cols], tag) for cols in halves]
-            for h in range(2):
-                quantize(grouped[h], codes[:, halves[h]], scales[:, halves[h]], fmt)
+        items = [("w", g, h) for g in range(4) for h in range(2)] + [("x", G, h) for G in range(2) for h in range(2)]
+
+        def item_copy(it):
+            kind, a, h = it
+            interleave(it, raw_t[(kind, a)][:, :, NT * h : NT * (h + 1)], "gw")
+
+        def item_quantize(it):
+            kind, a, h = it
+            cols = slice(NT * h, NT * (h + 1))
+            if kind == "w":
+                quantize(it, wq[:, a, cols], ws[:, a, cols], E4)
+            else:
+                quantize(it, xq[:, a, cols], xs[:, a, cols], E4)
 
         def evict(on_vector, dst, acc):
             if on_vector:
@@ -103,15 +113,14 @@ def tile_compute_gate_v_kernel(tc, input_word, hidden_states, Wx, bx, Wh, net, g
             else:
                 nc.scalar.mul(out=dst, in_=acc[:], mul=-1.0)
 
-        def activations(G, j):
-            halves = net_t[(G, j)][:].rearrange("p (c s w) -> p c s w", c=2, s=2)
-            for func in (ACT.Tanh, ACT.Square):
-                for s in range(2):
-                    nc.scalar.activation(out=halves[:, :, s, :], in_=halves[:, :, s, :], func=func, scale=0.5 if s == 0 else 1.0)
+        def activate(k, func):
+            halves = net_t[k][:].rearrange("p (c s w) -> p c s w", c=2, s=2)
+            for s in range(2):
+                nc.scalar.activation(out=halves[:, :, s, :], in_=halves[:, :, s, :], func=func, scale=0.5 if s == 0 else 1.0)
 
-        def multiply(G, j):
-            halves = net_t[(G, j)][:].rearrange("p (c s w) -> p c s w", c=2, s=2)
-            grads = dz[G][:, j, :].rearrange("p (c s w) -> p c s w", c=2, s=2)
+        def multiply(k):
+            halves = net_t[k][:].rearrange("p (c s w) -> p c s w", c=2, s=2)
+            grads = dz[k // 4][:, k % 4, :].rearrange("p (c s w) -> p c s w", c=2, s=2)
             for s in range(2):
                 nc.vector.scalar_tensor_tensor(
                     out=grads[:, :, 1 - s, :],
@@ -122,104 +131,167 @@ def tile_compute_gate_v_kernel(tc, input_word, hidden_states, Wx, bx, Wh, net, g
                     op1=ALU.mult,
                 )
 
-        def turn(G, j):
-            gf = grp.tile([P, PACK * KP], BF16, name="gf", tag="gf", align_bytes=64)
-            gf_words = gf[:].bitcast(F32)
+        def transposes(k):
             for b in range(2):
                 xt = psum.tile([P, NT], F32, name="xt", tag="bank")
                 for gg in range(2):
                     pos = (2 * b + gg) ^ 1
-                    words = dz[G][:, j, KP * pos : KP * (pos + 1)].bitcast(F32)
+                    words = dz[k // 4][:, k % 4, KP * pos : KP * (pos + 1)].bitcast(F32)
                     for u in range(2):
                         col = (2 * gg + u) * P
                         nc.tensor.transpose(xt[:, col : col + P], words[:, u : KP // 2 : 2], ident[:])
+                xt_t[(k, b)] = xt
+
+        def copy_out(k):
+            gf = grp.tile([P, PACK * KP], BF16, name="gf", tag="gf", align_bytes=64)
+            gf_words = gf[:].bitcast(F32)
+            for b in range(2):
                 nc.scalar.copy(
                     out=gf_words[:, NT * b : NT * (b + 1)].rearrange("p (g r u) -> p g r u", g=2, r=P, u=2),
-                    in_=xt[:].rearrange("p (g u r) -> p g r u", g=2, u=2, r=P),
+                    in_=xt_t[(k, b)][:].rearrange("p (g u r) -> p g r u", g=2, u=2, r=P),
                 )
-            nc.vector.quantize_mx(out=fq[:, PACK * G + j, :].bitcast(E5), scales=fs[:, PACK * G + j, :], in_=gf[:])
+            gf_t[k] = gf
 
-        def dx(G, j):
-            i = PACK * G + j
-            o = outp.tile([P, IN], F32, name="o", tag="o")
+        def quantize_turned(k):
+            nc.vector.quantize_mx(out=fq[:, k, :].bitcast(E5), scales=fs[:, k, :], in_=gf_t[k][:])
+
+        def dx_matmuls(k):
             for h in range(2):
                 cols = slice(NT * h, NT * (h + 1))
                 acc = psum.tile([P, NT], F32, name="acc", tag="bank")
                 for g in range(4):
                     nc.tensor.matmul_mx(
                         out=acc[:],
-                        lhsT=fq[:, i, P * g : P * (g + 1)].bitcast(E5),
-                        lhsT_scale=fs[:, i, P * g : P * (g + 1)],
+                        lhsT=fq[:, k, P * g : P * (g + 1)].bitcast(E5),
+                        lhsT_scale=fs[:, k, P * g : P * (g + 1)],
                         rhs=wq[:, g, cols].bitcast(E4),
                         rhs_scale=ws[:, g, cols],
                         start=(g == 0),
                         stop=(g == 3),
                     )
-                evict(h == 1 and i >= 2, o[:, cols], acc)
-            nc.sync.dma_start(out=out0_v[G, j], in_=o[:])
+                acc_t[("dx", k, h)] = acc
 
-        def dw(f):
-            for mm in range(4):
-                j0 = KP * f + P * mm
-                o = outp.tile([P, IN], F32, name="o", tag="o")
-                for h in range(2):
-                    cols = slice(NT * h, NT * (h + 1))
-                    acc = psum.tile([P, NT], F32, name="acc", tag="bank")
-                    for G in range(2):
-                        nc.tensor.matmul_mx(
-                            out=acc[:],
-                            lhsT=tq[:, G, j0 : j0 + P].bitcast(E5),
-                            lhsT_scale=ts[:, G, j0 : j0 + P],
-                            rhs=xq[:, G, cols].bitcast(E4),
-                            rhs_scale=xs[:, G, cols],
-                            start=(G == 0),
-                            stop=(G == 1),
-                        )
-                    evict(h == 1 and mm == 3, o[:, cols], acc)
-                nc.sync.dma_start(out=out1_v[4 * f + mm], in_=o[:])
+        def dx_out(k):
+            o = outp.tile([P, IN], F32, name="o", tag="o")
+            for h in range(2):
+                evict(h == 1 and k < 3, o[:, NT * h : NT * (h + 1)], acc_t[("dx", k, h)])
+            nc.sync.dma_start(out=out0_v[k // 4, k % 4], in_=o[:])
 
-        load_net(0, 0, 2)
-        load_w(0, 2)
-        load_g(0, 0)
-        load_net(0, 1, 1)
-        load_w(1, 1)
-        load_g(0, 1)
-        load_net(0, 2, 1)
-        load_w(2, 1)
-        load_g(0, 2)
-        load_net(0, 3, 1)
-        load_w(3, 1)
-        load_g(0, 3)
-        load_net(1, 0, 1)
-        load_g(1, 0)
-        load_net(1, 1, 1)
-        load_g(1, 1)
-
-        for g in range(4):
-            quantize_pair(w_t[g], wq[:, g, :], ws[:, g, :], E4, "gw")
-
-        for G in range(2):
-            for j in range(4):
-                activations(G, j)
-                multiply(G, j)
-                turn(G, j)
-                dx(G, j)
-                if (G, j) == (0, 0):
-                    load_x(0)
-                    load_net(1, 2, 1)
-                    load_g(1, 2)
-                if (G, j) == (0, 1):
-                    load_x(1)
-                    load_net(1, 3, 1)
-                    load_g(1, 3)
-                if (G, j) == (0, 3):
-                    quantize_pair(x_t[0], xq[:, 0, :], xs[:, 0, :], E4, "gw")
-                if (G, j) == (1, 1):
-                    quantize_pair(x_t[1], xq[:, 1, :], xs[:, 1, :], E4, "gw")
-
-        for f in range(4):
+        def column_copy(f):
             pos = f ^ 1
-            grouped = [interleave(dz[G][:, :, KP * pos : KP * (pos + 1)], "gt") for G in range(2)]
             for G in range(2):
-                quantize(grouped[G], tq[:, G, KP * f : KP * (f + 1)], ts[:, G, KP * f : KP * (f + 1)], E5)
-            dw(f)
+                interleave(("t", G, f), dz[G][:, :, KP * pos : KP * (pos + 1)], "gt")
+
+        def column_quantize(f):
+            for G in range(2):
+                quantize(("t", G, f), tq[:, G, KP * f : KP * (f + 1)], ts[:, G, KP * f : KP * (f + 1)], E5)
+
+        def dw_matmuls(f, mm):
+            j0 = KP * f + P * mm
+            for h in range(2):
+                cols = slice(NT * h, NT * (h + 1))
+                acc = psum.tile([P, NT], F32, name="acc", tag="bank")
+                for G in range(2):
+                    nc.tensor.matmul_mx(
+                        out=acc[:],
+                        lhsT=tq[:, G, j0 : j0 + P].bitcast(E5),
+                        lhsT_scale=ts[:, G, j0 : j0 + P],
+                        rhs=xq[:, G, cols].bitcast(E4),
+                        rhs_scale=xs[:, G, cols],
+                        start=(G == 0),
+                        stop=(G == 1),
+                    )
+                acc_t[("dw", f, mm, h)] = acc
+
+        def dw_out(f, mm):
+            o = outp.tile([P, IN], F32, name="o", tag="o")
+            for h in range(2):
+                evict(False, o[:, NT * h : NT * (h + 1)], acc_t[("dw", f, mm, h)])
+            nc.sync.dma_start(out=out1_v[4 * f + mm], in_=o[:])
+
+        load_net(0, 2)
+        load_rows("w", 0, w_v, 2)
+        load_g(0)
+        load_net(1, 1)
+        load_rows("w", 1, w_v, 1)
+        for k in range(2, 4):
+            load_net(k, 1)
+            load_g(k - 1)
+            load_rows("w", k, w_v, 1)
+        for k in range(4, 6):
+            load_net(k, 1)
+            load_g(k - 1)
+        load_g(5)
+
+        item_copy(items[0])
+        item_copy(items[1])
+        item_quantize(items[0])
+        item_quantize(items[1])
+        for k in range(LEAD):
+            activate(k, ACT.Tanh)
+            activate(k, ACT.Square)
+
+        taken = 2
+        wait_matmul = []
+        wait_out = []
+        for k in range(8):
+            mine = items[taken : taken + FILL[k]]
+            taken += FILL[k]
+            early = 1 <= k < 8 - LEAD
+            if early:
+                copy_out(k - 1)
+            if k > 0 and len(mine) > 0:
+                item_copy(mine[0])
+            multiply(k)
+            transposes(k)
+            if k == 0:
+                item_copy(mine[0])
+            if len(mine) > 1:
+                item_copy(mine[1])
+            if early:
+                quantize_turned(k - 1)
+                wait_matmul.append(k - 1)
+            for it in mine:
+                item_quantize(it)
+            if k >= 8 - LEAD:
+                copy_out(k - 1)
+                quantize_turned(k - 1)
+                wait_matmul.append(k - 1)
+            if k < 2:
+                load_rows("x", k, x_v, 1)
+                load_net(6 + k, 1)
+                load_g(6 + k)
+            if k + LEAD < 8:
+                activate(k + LEAD, ACT.Tanh)
+            for b in wait_out:
+                dx_out(b)
+            wait_out = []
+            if taken >= 8:
+                for b in wait_matmul[:2]:
+                    dx_matmuls(b)
+                    wait_out.append(b)
+                wait_matmul = wait_matmul[2:]
+            if k + LEAD < 8:
+                activate(k + LEAD, ACT.Square)
+
+        copy_out(7)
+        column_copy(0)
+        for b in wait_out:
+            dx_out(b)
+        quantize_turned(7)
+        column_quantize(0)
+        dx_matmuls(7)
+        column_copy(1)
+        column_quantize(1)
+        for f in range(4):
+            for mm in range(4):
+                dw_matmuls(f, mm)
+                if f == 0 and mm == 1:
+                    dx_out(7)
+                if mm == 1 and f + 2 < 4:
+                    column_copy(f + 2)
+                if mm >= 1:
+                    dw_out(f, mm - 1)
+                if mm == 2 and f + 2 < 4:
+                    column_quantize(f + 2)
+            dw_out(f, 3)

@@ -87,7 +87,9 @@ def tile_compute_gate_v_kernel(tc, input_word, hidden_states, Wx, bx, Wh, net, g
 
         def interleave(key, src, tag):
             grouped = grp.tile([P, NT, PACK], BF16, name=tag, tag=tag, align_bytes=64)
-            nc.vector.tensor_copy(out=grouped[:], in_=src.rearrange("p j w -> p w j"))
+            nc.vector.tensor_copy(
+                out=grouped[:].rearrange("p (c i) j -> p c j i", i=4), in_=src.rearrange("p j (c i) -> p c j i", i=4)
+            )
             grouped_t[key] = grouped
 
         def quantize(key, codes, scales, fmt):

@@ -87,9 +87,7 @@ def tile_compute_gate_v_kernel(tc, input_word, hidden_states, Wx, bx, Wh, net, g
 
         def interleave(key, src, tag):
             grouped = grp.tile([P, NT, PACK], BF16, name=tag, tag=tag, align_bytes=64)
-            nc.vector.tensor_copy(
-                out=grouped[:].rearrange("p (c i) j -> p c j i", i=4), in_=src.rearrange("p j (c i) -> p c j i", i=4)
-            )
+            nc.vector.tensor_copy(out=grouped[:], in_=src.rearrange("p j w -> p w j"))
             grouped_t[key] = grouped
 
         def quantize(key, codes, scales, fmt):
@@ -206,7 +204,7 @@ def tile_compute_gate_v_kernel(tc, input_word, hidden_states, Wx, bx, Wh, net, g
                 acc_t[("dw", f, mm, h)] = acc
 
         def dw_out(f, mm):
-            o = outp.tile([P, IN], F32, name="o", tag="o")
+            o = raw.tile([P, IN], F32, name="o_dw", tag="raw")
             for h in range(2):
                 evict(False, o[:, NT * h : NT * (h + 1)], acc_t[("dw", f, mm, h)])
             nc.sync.dma_start(out=out1_v[4 * f + mm], in_=o[:])

@@ -87,7 +87,9 @@ def tile_compute_gate_v_kernel(tc, input_word, hidden_states, Wx, bx, Wh, net, g
 
         def interleave(key, src, tag):
             grouped = grp.tile([P, NT, PACK], BF16, name=tag, tag=tag, align_bytes=64)
-            nc.vector.tensor_copy(out=grouped[:], in_=src.rearrange("p j w -> p w j"))
+            nc.vector.tensor_copy(
+                out=grouped[:].rearrange("p (c i) j -> p c j i", i=4), in_=src.rearrange("p j (c i) -> p c j i", i=4)
+            )
             grouped_t[key] = grouped
 
         def quantize(key, codes, scales, fmt):
@@ -146,10 +148,12 @@ def tile_compute_gate_v_kernel(tc, input_word, hidden_states, Wx, bx, Wh, net, g
             gf = grp.tile([P, PACK * KP], BF16, name="gf", tag="gf", align_bytes=64)
             gf_words = gf[:].bitcast(F32)
             for b in range(2):
-                nc.scalar.copy(
-                    out=gf_words[:, NT * b : NT * (b + 1)].rearrange("p (g r u) -> p g r u", g=2, r=P, u=2),
-                    in_=xt_t[(k, b)][:].rearrange("p (g u r) -> p g r u", g=2, u=2, r=P),
-                )
+                dst = gf_words[:, NT * b : NT * (b + 1)].rearrange("p (g r u) -> p g r u", g=2, r=P, u=2)
+                src = xt_t[(k, b)][:].rearrange("p (g u r) -> p g r u", g=2, u=2, r=P)
+                if b == 1 and k < 3:
+                    nc.vector.tensor_copy(out=dst, in_=src)
+                else:
+                    nc.scalar.copy(out=dst, in_=src)
             gf_t[k] = gf
 
         def quantize_turned(k):
@@ -206,7 +210,7 @@ def tile_compute_gate_v_kernel(tc, input_word, hidden_states, Wx, bx, Wh, net, g
         def dw_out(f, mm):
             o = raw.tile([P, IN], F32, name="o_dw", tag="raw")
             for h in range(2):
-                evict(False, o[:, NT * h : NT * (h + 1)], acc_t[("dw", f, mm, h)])
+                evict(h == 1 and mm == 3, o[:, NT * h : NT * (h + 1)], acc_t[("dw", f, mm, h)])
             nc.sync.dma_start(out=out1_v[4 * f + mm], in_=o[:])
 
         load_net(0, 2)

from contextlib import ExitStack

import concourse.mybir as mybir
from concourse.masks import make_identity

B, IN, J = 1024, 1024, 2048
FLOPS = 2 * 2 * B * J * IN
BYTES = B * J * 4 + B * J * 2 + J * IN * 2 + B * IN * 2 + B * IN * 4 + J * IN * 4

F32 = mybir.dt.float32
BF16 = mybir.dt.bfloat16
U32 = mybir.dt.uint32
U8 = mybir.dt.uint8
E4 = mybir.dt.float8_e4m3fn_x4
E5 = mybir.dt.float8_e5m2_x4
ACT = mybir.ActivationFunctionType
ALU = mybir.AluOpType

P = 128
PACK = 4
KP = P * PACK
NT = 512
LEAD = 2
FILL = [1, 2, 2, 1, 1, 2, 1, 0]


def tile_compute_gate_v_kernel(tc, input_word, hidden_states, Wx, bx, Wh, net, grad_out, out_0, out_1):
    nc = tc.nc

    net_v = net.rearrange("(g p j) c h -> g j p (c h)", g=2, p=P, j=PACK)
    grad_v = grad_out.rearrange("(g p j) c h -> g j p (c h)", g=2, p=P, j=PACK)
    x_v = input_word.rearrange("(g p j) n -> g p j n", g=2, p=P, j=PACK)
    w_v = Wx.rearrange("c (a p j) n -> (c a) p j n", a=2, p=P, j=PACK)
    out0_v = out_0.rearrange("(g r j) n -> g j r n", g=2, r=P, j=PACK)
    out1_v = out_1.rearrange("c (m p) n -> (c m) p n", p=P)

    with ExitStack() as ctx:
        raw = ctx.enter_context(tc.tile_pool(name="raw", bufs=10))
        keep = ctx.enter_context(tc.tile_pool(name="keep", bufs=1))
        grp = ctx.enter_context(tc.tile_pool(name="grp", bufs=2))
        outp = ctx.enter_context(tc.tile_pool(name="outp", bufs=4))
        psum = ctx.enter_context(tc.psum_pool(name="psum", bufs=8))

        xq = keep.tile([P, 2, IN], U32, name="xq", align_bytes=64)
        xs = keep.tile([P, 2, IN], U8, name="xs", align_bytes=64)
        wq = keep.tile([P, 4, IN], U32, name="wq", align_bytes=64)
        ws = keep.tile([P, 4, IN], U8, name="ws", align_bytes=64)
        tq = keep.tile([P, 2, J], U32, name="tq", align_bytes=64)
        ts = keep.tile([P, 2, J], U8, name="ts", align_bytes=64)
        fq = keep.tile([P, 8, KP], U32, name="fq", align_bytes=64)
        fs = keep.tile([P, 8, KP], U8, name="fs", align_bytes=64)
        dz0 = keep.tile([P, PACK, J], BF16, name="dz0", align_bytes=64)
        dz1 = keep.tile([P, PACK, J], BF16, name="dz1", align_bytes=64)
        dz = [dz0, dz1]
        ident = keep.tile([P, P], F32, name="ident")
        warm = keep.tile([P, 1], F32, name="warm")

        nc.vector.memset(warm[:], 0.0)
        nc.scalar.activation(out=warm[:], in_=warm[:], func=ACT.Tanh)
        make_identity(nc, ident[:])

        ctx.enter_context(tc.manual_schedule())

        net_t = {}
        raw_t = {}
        grouped_t = {}
        xt_t = {}
        gf_t = {}
        acc_t = {}

        def load_net(k, pieces):
            t = raw.tile([P, J], F32, name="net_t", tag="raw")
            step = J // pieces
            for i in range(pieces):
                nc.sync.dma_start(out=t[:, step * i : step * (i + 1)], in_=net_v[k // 4, k % 4][:, step * i : step * (i + 1)])
            net_t[k] = t

        def load_g(k):
            nc.sync.dma_start(out=dz[k // 4][:, k % 4, :], in_=grad_v[k // 4, k % 4])

        def load_rows(kind, a, view, pieces):
            t = raw.tile([P, PACK, IN], BF16, name="rows_t", tag="raw")
            step = IN // pieces
            for i in range(pieces):
                nc.sync.dma_start(out=t[:, :, step * i : step * (i + 1)], in_=view[a][:, :, step * i : step * (i + 1)])
            raw_t[(kind, a)] = t

        def interleave(key, src, tag):
            grouped = grp.tile([P, NT, PACK], BF16, name=tag, tag=tag, align_bytes=64)
            nc.vector.tensor_copy(
                out=grouped[:].rearrange("p (c i) j -> p c j i", i=4), in_=src.rearrange("p j (c i) -> p c j i", i=4)
            )
            grouped_t[key] = grouped

        def quantize(key, codes, scales, fmt):
            nc.vector.quantize_mx(out=codes.bitcast(fmt), scales=scales, in_=grouped_t[key][:].rearrange("p w j -> p (w j)"))

        items = [("w", g, h) for g in range(4) for h in range(2)] + [("x", G, h) for G in range(2) for h in range(2)]

        def item_copy(it):
            kind, a, h = it
            interleave(it, raw_t[(kind, a)][:, :, NT * h : NT * (h + 1)], "gw")

        def item_quantize(it):
            kind, a, h = it
            cols = slice(NT * h, NT * (h + 1))
            if kind == "w":
                quantize(it, wq[:, a, cols], ws[:, a, cols], E4)
            else:
                quantize(it, xq[:, a, cols], xs[:, a, cols], E4)

        def evict(on_vector, dst, acc):
            if on_vector:
                nc.vector.tensor_scalar_mul(out=dst, in0=acc[:], scalar1=-1.0)
            else:
                nc.scalar.mul(out=dst, in_=acc[:], mul=-1.0)

        def activate(k, func):
            halves = net_t[k][:].rearrange("p (c s w) -> p c s w", c=2, s=2)
            for s in range(2):
                nc.scalar.activation(out=halves[:, :, s, :], in_=halves[:, :, s, :], func=func, scale=0.5 if s == 0 else 1.0)

        def multiply(k):
            halves = net_t[k][:].rearrange("p (c s w) -> p c s w", c=2, s=2)
            grads = dz[k // 4][:, k % 4, :].rearrange("p (c s w) -> p c s w", c=2, s=2)
            for s in range(2):
                nc.vector.scalar_tensor_tensor(
                    out=grads[:, :, 1 - s, :],
                    in0=halves[:, :, s, :],
                    scalar=0.25 if s == 0 else 1.0,
                    in1=grads[:, :, 1 - s, :],
                    op0=ALU.subtract,
                    op1=ALU.mult,
                )

        def transposes(k):
            for b in range(2):
                xt = psum.tile([P, NT], F32, name="xt", tag="bank")
                for gg in range(2):
                    pos = (2 * b + gg) ^ 1
                    words = dz[k // 4][:, k % 4, KP * pos : KP * (pos + 1)].bitcast(F32)
                    for u in range(2):
                        col = (2 * gg + u) * P
                        nc.tensor.transpose(xt[:, col : col + P], words[:, u : KP // 2 : 2], ident[:])
                xt_t[(k, b)] = xt

        def copy_out(k):
            gf = grp.tile([P, PACK * KP], BF16, name="gf", tag="gf", align_bytes=64)
            gf_words = gf[:].bitcast(F32)
            for b in range(2):
                dst = gf_words[:, NT * b : NT * (b + 1)].rearrange("p (g r u) -> p g r u", g=2, r=P, u=2)
                src = xt_t[(k, b)][:].rearrange("p (g u r) -> p g r u", g=2, u=2, r=P)
                if b == 1 and k < 3:
                    nc.vector.tensor_copy(out=dst, in_=src)
                else:
                    nc.scalar.copy(out=dst, in_=src)
            gf_t[k] = gf

        def quantize_turned(k):
            nc.vector.quantize_mx(out=fq[:, k, :].bitcast(E5), scales=fs[:, k, :], in_=gf_t[k][:])

        def dx_matmuls(k):
            for h in range(2):
                cols = slice(NT * h, NT * (h + 1))
                acc = psum.tile([P, NT], F32, name="acc", tag="bank")
                for g in range(4):
                    nc.tensor.matmul_mx(
                        out=acc[:],
                        lhsT=fq[:, k, P * g : P * (g + 1)].bitcast(E5),
                        lhsT_scale=fs[:, k, P * g : P * (g + 1)],
                        rhs=wq[:, g, cols].bitcast(E4),
                        rhs_scale=ws[:, g, cols],
                        start=(g == 0),
                        stop=(g == 3),
                    )
                acc_t[("dx", k, h)] = acc

        def dx_out(k):
            o = outp.tile([P, IN], F32, name="o", tag="o")
            for h in range(2):
                evict(h == 1 and k < 3, o[:, NT * h : NT * (h + 1)], acc_t[("dx", k, h)])
            nc.sync.dma_start(out=out0_v[k // 4, k % 4], in_=o[:])

        def column_copy(f):
            pos = f ^ 1
            for G in range(2):
                interleave(("t", G, f), dz[G][:, :, KP * pos : KP * (pos + 1)], "gt")

        def column_quantize(f):
            for G in range(2):
                quantize(("t", G, f), tq[:, G, KP * f : KP * (f + 1)], ts[:, G, KP * f : KP * (f + 1)], E5)

        def dw_matmuls(f, mm):
            j0 = KP * f + P * mm
            for h in range(2):
                cols = slice(NT * h, NT * (h + 1))
                acc = psum.tile([P, NT], F32, name="acc", tag="bank")
                for G in range(2):
                    nc.tensor.matmul_mx(
                        out=acc[:],
                        lhsT=tq[:, G, j0 : j0 + P].bitcast(E5),
                        lhsT_scale=ts[:, G, j0 : j0 + P],
                        rhs=xq[:, G, cols].bitcast(E4),
                        rhs_scale=xs[:, G, cols],
                        start=(G == 0),
                        stop=(G == 1),
                    )
                acc_t[("dw", f, mm, h)] = acc

        def dw_out(f, mm):
            o = raw.tile([P, IN], F32, name="o_dw", tag="raw")
            for h in range(2):
                evict(h == 1 and mm == 3, o[:, NT * h : NT * (h + 1)], acc_t[("dw", f, mm, h)])
            nc.sync.dma_start(out=out1_v[4 * f + mm], in_=o[:])

        load_net(0, 2)
        load_rows("w", 0, w_v, 2)
        load_g(0)
        load_net(1, 1)
        load_rows("w", 1, w_v, 1)
        for k in range(2, 4):
            load_net(k, 1)
            load_g(k - 1)
            load_rows("w", k, w_v, 1)
        for k in range(4, 6):
            load_net(k, 1)
            load_g(k - 1)
        load_g(5)

        item_copy(items[0])
        item_copy(items[1])
        item_quantize(items[0])
        item_quantize(items[1])
        for k in range(LEAD):
            activate(k, ACT.Tanh)
            activate(k, ACT.Square)

        taken = 2
        wait_matmul = []
        wait_out = []
        for k in range(8):
            mine = items[taken : taken + FILL[k]]
            taken += FILL[k]
            early = 1 <= k < 8 - LEAD
            if early:
                copy_out(k - 1)
            if k > 0 and len(mine) > 0:
                item_copy(mine[0])
            multiply(k)
            transposes(k)
            if k == 0:
                item_copy(mine[0])
            if len(mine) > 1:
                item_copy(mine[1])
            if early:
                quantize_turned(k - 1)
                wait_matmul.append(k - 1)
            for it in mine:
                item_quantize(it)
            if k >= 8 - LEAD:
                copy_out(k - 1)
                quantize_turned(k - 1)
                wait_matmul.append(k - 1)
            if k < 2:
                load_rows("x", k, x_v, 1)
                load_net(6 + k, 1)
                load_g(6 + k)
            if k + LEAD < 8:
                activate(k + LEAD, ACT.Tanh)
            for b in wait_out:
                dx_out(b)
            wait_out = []
            if taken >= 8:
                for b in wait_matmul[:2]:
                    dx_matmuls(b)
                    wait_out.append(b)
                wait_matmul = wait_matmul[2:]
            if k + LEAD < 8:
                activate(k + LEAD, ACT.Square)

        copy_out(7)
        column_copy(0)
        for b in wait_out:
            dx_out(b)
        quantize_turned(7)
        column_quantize(0)
        dx_matmuls(7)
        column_copy(1)
        column_quantize(1)
        for f in range(4):
            for mm in range(4):
                dw_matmuls(f, mm)
                if f == 0 and mm == 1:
                    dx_out(7)
                if mm == 1 and f + 2 < 4:
                    column_copy(f + 2)
                if mm >= 1:
                    dw_out(f, mm - 1)
                if mm == 2 and f + 2 < 4:
                    column_quantize(f + 2)
            dw_out(f, 3)
